import numpy as np
import ml_dtypes


def mxq(x, axis, fmt="e4m3"):
    dtype, down = {"e4m3": (ml_dtypes.float8_e4m3fn, 7), "e5m2": (ml_dtypes.float8_e5m2, 14)}[fmt]
    v = np.moveaxis(np.asarray(x, np.float32).astype(ml_dtypes.bfloat16).astype(np.float64), axis, -1)
    blocks = v.reshape(v.shape[:-1] + (-1, 32))
    amax = np.abs(blocks).max(-1, keepdims=True)
    byte = np.maximum(np.where(amax > 0, np.frexp(amax)[1] - 1 + 127, 0) - down, 1)
    scale = np.exp2(byte - 127.0)
    codes = (blocks / scale).astype(np.float32).astype(dtype).astype(np.float64)
    return np.moveaxis((codes * scale).reshape(v.shape), -1, axis)


WIDE = False


def mx_kscale(k):
    if not WIDE:
        return np.ones(k)
    levels = np.array([10, -10, 5, -5, 0])
    a = np.random.permutation(np.resize(levels, k // 512 * 4)).reshape(k // 512, 4)
    idx = np.arange(k)
    return np.exp2(a[idx // 512, idx % 128 // 32])


BF16 = ml_dtypes.bfloat16


def bf(x):
    return np.asarray(x, np.float32).astype(BF16)


def f64(x):
    return np.asarray(x).astype(np.float64)


B, I, C, K, L, S0, S1, S2, S3, S4 = 2, 8, 512, 7, 5, 16, 12, 8, 6, 4
P = S2 * S2


def setup_inputs():
    t = mx_kscale(C)
    return {"q": bf(np.random.standard_normal((B, I, C))),
            "feats": bf(np.random.standard_normal((B, C, S2, S2)) * t[:, None, None]),
            "po_w": bf(np.random.standard_normal((C, C)) / np.sqrt(C) / t),
            "po_b": bf(np.random.standard_normal(C) * 0.3)}


def reference(q, feats, po_w, po_b):
    m = f64(q)[:, :, :, None] * f64(feats).reshape(B, C, P)[:, None]
    o = (mxq(f64(po_w), 1, "e4m3") @ mxq(m, 2, "e4m3")) + f64(po_b)[:, None]
    return o.reshape(B, I, C, S2, S2)

@@ -1,0 +1,136 @@
+from contextlib import ExitStack
+
+import concourse.mybir as mybir
+from concourse.masks import make_identity
+
+F32 = mybir.dt.float32
+BF16 = mybir.dt.bfloat16
+U32 = mybir.dt.uint32
+U8 = mybir.dt.uint8
+FP8X4 = mybir.dt.float8_e4m3fn_x4
+
+P = 128
+PACK = 4
+HALVES = 2
+
+IMAGES = 2
+INSTANCES = 8
+CHANNELS = 512
+PIXELS = 64
+ROWS = IMAGES * INSTANCES
+O_TILES = CHANNELS // P
+GROUP = 4
+GROUPS = ROWS // GROUP
+GROUP_COLS = GROUP * PIXELS
+
+FLOPS = 2 * ROWS * PIXELS * CHANNELS * CHANNELS
+
+
+def tile_rpn_modulator_pb_s_kernel(tc, q, feats, po_w, po_b, out):
+    nc = tc.nc
+    with ExitStack() as ctx:
+        consts = ctx.enter_context(tc.tile_pool(name="consts", bufs=1))
+        weights = ctx.enter_context(tc.tile_pool(name="weights", bufs=O_TILES))
+        columns = ctx.enter_context(tc.tile_pool(name="columns", bufs=GROUPS))
+        turned = ctx.enter_context(tc.psum_pool(name="turned", bufs=2))
+        sums = ctx.enter_context(tc.psum_pool(name="sums", bufs=6))
+
+        identity = consts.tile([P, P], F32)
+        make_identity(nc, identity[:])
+
+        w_view = po_w.rearrange("(m t) c -> m t c", t=O_TILES)
+        w_rows_all = []
+        for t in range(O_TILES):
+            w_rows = weights.tile([P, CHANNELS], BF16)
+            nc.sync.dma_start(out=w_rows[:], in_=w_view[:, t, :])
+            w_rows_all.append(w_rows)
+
+        feats_rows = consts.tile([P, IMAGES, PACK * PIXELS], BF16)
+        nc.scalar.dma_start(
+            out=feats_rows[:], in_=feats.rearrange("b (p j) y x -> p b (j y x)", j=PACK)
+        )
+        q_cols = consts.tile([P, ROWS, PACK], BF16)
+        nc.scalar.dma_start(out=q_cols[:], in_=q.rearrange("b i (p j) -> p (b i) j", j=PACK))
+        bias_bf16 = consts.tile([P, O_TILES], BF16)
+        nc.scalar.dma_start(out=bias_bf16[:], in_=po_b.rearrange("(m t) -> m t", t=O_TILES))
+        bias = consts.tile([P, O_TILES], F32)
+        nc.gpsimd.tensor_copy(out=bias[:], in_=bias_bf16[:])
+
+        feats_grouped = consts.tile([P, IMAGES, PIXELS, PACK], BF16)
+        nc.vector.tensor_copy(
+            out=feats_grouped[:], in_=feats_rows[:].rearrange("p b (j w) -> p b w j", j=PACK)
+        )
+
+        w_codes_all = []
+        w_scales_all = []
+        for t in range(O_TILES):
+            w_words = w_rows_all[t][:].bitcast(F32).rearrange("m (p u) -> m u p", u=HALVES)
+            w_turned = turned.tile([P, HALVES, P], F32)
+            for u in range(HALVES):
+                nc.tensor.transpose(w_turned[:, u, :], w_words[:, u, :], identity[:])
+            w_grouped = weights.tile([P, P * PACK], BF16, align_bytes=64)
+            nc.scalar.copy(
+                out=w_grouped[:].bitcast(F32).rearrange("p (m u) -> p m u", u=HALVES),
+                in_=w_turned[:].rearrange("p u m -> p m u"),
+            )
+            w_codes = weights.tile([P, P], U32, align_bytes=64)
+            w_scales = weights.tile([P, P], U8, align_bytes=64)
+            nc.vector.quantize_mx(
+                out=w_codes[:].bitcast(FP8X4), scales=w_scales[:], in_=w_grouped[:]
+            )
+            w_codes_all.append(w_codes)
+            w_scales_all.append(w_scales)
+
+        m_codes_all = []
+        m_scales_all = []
+        for g in range(GROUPS):
+            b = g * GROUP // INSTANCES
+            shape = [P, GROUP, PIXELS, PACK]
+            m_grouped = columns.tile(shape, BF16, align_bytes=64)
+            nc.vector.tensor_tensor(
+                out=m_grouped[:],
+                in0=feats_grouped[:, b].unsqueeze(1).to_broadcast(shape),
+                in1=q_cols[:, g * GROUP : (g + 1) * GROUP, :].unsqueeze(2).to_broadcast(shape),
+                op=mybir.AluOpType.mult,
+            )
+            m_codes = columns.tile([P, GROUP_COLS], U32, align_bytes=64)
+            m_scales = columns.tile([P, GROUP_COLS], U8, align_bytes=64)
+            nc.vector.quantize_mx(
+                out=m_codes[:].bitcast(FP8X4),
+                scales=m_scales[:],
+                in_=m_grouped[:].rearrange("p i w j -> p (i w j)"),
+            )
+            m_codes_all.append(m_codes)
+            m_scales_all.append(m_scales)
+
+        out_view = out.rearrange("b i (m t) y x -> m (b i) (t y x)", t=O_TILES)
+        for g in range(GROUPS):
+            result = columns.tile([P, GROUP, O_TILES, PIXELS], F32)
+            for t in range(O_TILES):
+                acc = sums.tile([P, GROUP_COLS], F32)
+                nc.tensor.matmul_mx(
+                    out=acc[:],
+                    lhsT=w_codes_all[t][:].bitcast(FP8X4),
+                    lhsT_scale=w_scales_all[t][:],
+                    rhs=m_codes_all[g][:].bitcast(FP8X4),
+                    rhs_scale=m_scales_all[g][:],
+                    start=True,
+                    stop=True,
+                )
+                acc_view = acc[:].rearrange("m (i w) -> m i w", w=PIXELS)
+                if t % 2 == 0:
+                    nc.scalar.activation(
+                        out=result[:, :, t, :],
+                        in_=acc_view,
+                        func=mybir.ActivationFunctionType.Identity,
+                        bias=bias[:, t : t + 1],
+                        scale=1.0,
+                    )
+                else:
+                    nc.vector.tensor_scalar_add(
+                        out=result[:, :, t, :], in0=acc_view, scalar1=bias[:, t : t + 1]
+                    )
+            nc.sync.dma_start(
+                out=out_view[:, g * GROUP : (g + 1) * GROUP, :],
+                in_=result[:].rearrange("m i t w -> m i (t w)"),
+            )

@@ -49,8 +49,9 @@ def tile_rpn_modulator_pb_s_kernel(tc, q, feats, po_w, po_b, out):
         nc.scalar.dma_start(
             out=feats_rows[:], in_=feats.rearrange("b (p j) y x -> p b (j y x)", j=PACK)
         )
-        q_cols = consts.tile([P, ROWS, PACK], BF16)
-        nc.scalar.dma_start(out=q_cols[:], in_=q.rearrange("b i (p j) -> p (b i) j", j=PACK))
+        q_rows = consts.tile([P, CHANNELS], BF16)
+        nc.vector.memset(q_rows[:], 0.0)
+        nc.scalar.dma_start(out=q_rows[0:ROWS, :], in_=q.rearrange("b i c -> (b i) c"))
         bias_bf16 = consts.tile([P, O_TILES], BF16)
         nc.scalar.dma_start(out=bias_bf16[:], in_=po_b.rearrange("(m t) -> m t", t=O_TILES))
         bias = consts.tile([P, O_TILES], F32)
@@ -59,6 +60,18 @@ def tile_rpn_modulator_pb_s_kernel(tc, q, feats, po_w, po_b, out):
         feats_grouped = consts.tile([P, IMAGES, PIXELS, PACK], BF16)
         nc.vector.tensor_copy(
             out=feats_grouped[:], in_=feats_rows[:].rearrange("p b (j w) -> p b w j", j=PACK)
+        )
+
+        q_words = q_rows[:].bitcast(F32).rearrange("r (p u) -> r u p", u=HALVES)
+        q_turned = turned.tile([P, HALVES, P], F32, tag="w_turned")
+        for u in range(HALVES):
+            nc.tensor.transpose(q_turned[:, u, :], q_words[:, u, :], identity[:])
+        q_cols = consts.tile([P, ROWS, PACK], BF16)
+        nc.vector.tensor_copy(
+            out=q_cols[:].rearrange("p r j -> p (r j)").bitcast(F32).rearrange(
+                "p (r u) -> p r u", u=HALVES
+            ),
+            in_=q_turned[:, :, 0:ROWS].rearrange("p u r -> p r u"),
         )
 
         w_codes_all = []

@@ -32,8 +32,9 @@ def tile_rpn_modulator_pb_s_kernel(tc, q, feats, po_w, po_b, out):
         consts = ctx.enter_context(tc.tile_pool(name="consts", bufs=1))
         weights = ctx.enter_context(tc.tile_pool(name="weights", bufs=O_TILES))
         columns = ctx.enter_context(tc.tile_pool(name="columns", bufs=GROUPS))
-        turned = ctx.enter_context(tc.psum_pool(name="turned", bufs=2))
-        sums = ctx.enter_context(tc.psum_pool(name="sums", bufs=6))
+        turned = ctx.enter_context(tc.psum_pool(name="turned", bufs=4))
+        sums = ctx.enter_context(tc.psum_pool(name="sums", bufs=4))
+        ctx.enter_context(tc.manual_schedule())
 
         identity = consts.tile([P, P], F32)
         make_identity(nc, identity[:])
@@ -45,13 +46,18 @@ def tile_rpn_modulator_pb_s_kernel(tc, q, feats, po_w, po_b, out):
             nc.sync.dma_start(out=w_rows[:], in_=w_view[:, t, :])
             w_rows_all.append(w_rows)
 
+        q_rows = consts.tile([P, CHANNELS], BF16)
+        for k in range(2):
+            nc.scalar.dma_start(
+                out=q_rows[k * ROWS : (k + 1) * ROWS, :], in_=q.rearrange("b i c -> (b i) c")
+            )
+        nc.vector.memset(q_rows[2 * ROWS : 4 * ROWS, :], 0.0)
+        nc.vector.memset(q_rows[4 * ROWS : P, :], 0.0)
         feats_rows = consts.tile([P, IMAGES, PACK * PIXELS], BF16)
         nc.scalar.dma_start(
-            out=feats_rows[:], in_=feats.rearrange("b (p j) y x -> p b (j y x)", j=PACK)
+            out=feats_rows[:].rearrange("p b (u r) -> p (b u) r", u=HALVES),
+            in_=feats.rearrange("b (u p e) y x -> p (b u) (e y x)", u=HALVES, e=2),
         )
-        q_rows = consts.tile([P, CHANNELS], BF16)
-        nc.vector.memset(q_rows[:], 0.0)
-        nc.scalar.dma_start(out=q_rows[0:ROWS, :], in_=q.rearrange("b i c -> (b i) c"))
         bias_bf16 = consts.tile([P, O_TILES], BF16)
         nc.scalar.dma_start(out=bias_bf16[:], in_=po_b.rearrange("(m t) -> m t", t=O_TILES))
         bias = consts.tile([P, O_TILES], F32)
@@ -62,41 +68,25 @@ def tile_rpn_modulator_pb_s_kernel(tc, q, feats, po_w, po_b, out):
             out=feats_grouped[:], in_=feats_rows[:].rearrange("p b (j w) -> p b w j", j=PACK)
         )
 
-        q_words = q_rows[:].bitcast(F32).rearrange("r (p u) -> r u p", u=HALVES)
-        q_turned = turned.tile([P, HALVES, P], F32, tag="w_turned")
-        for u in range(HALVES):
-            nc.tensor.transpose(q_turned[:, u, :], q_words[:, u, :], identity[:])
-        q_cols = consts.tile([P, ROWS, PACK], BF16)
-        nc.vector.tensor_copy(
-            out=q_cols[:].rearrange("p r j -> p (r j)").bitcast(F32).rearrange(
-                "p (r u) -> p r u", u=HALVES
-            ),
-            in_=q_turned[:, :, 0:ROWS].rearrange("p u r -> p r u"),
-        )
-
-        w_codes_all = []
-        w_scales_all = []
-        for t in range(O_TILES):
-            w_words = w_rows_all[t][:].bitcast(F32).rearrange("m (p u) -> m u p", u=HALVES)
-            w_turned = turned.tile([P, HALVES, P], F32)
+        def turn(rows):
+            words = rows[:].bitcast(F32).rearrange("r (u p) -> r u p", u=HALVES)
+            halves = turned.tile([P, HALVES, P], F32)
             for u in range(HALVES):
-                nc.tensor.transpose(w_turned[:, u, :], w_words[:, u, :], identity[:])
-            w_grouped = weights.tile([P, P * PACK], BF16, align_bytes=64)
-            nc.scalar.copy(
-                out=w_grouped[:].bitcast(F32).rearrange("p (m u) -> p m u", u=HALVES),
-                in_=w_turned[:].rearrange("p u m -> p m u"),
-            )
-            w_codes = weights.tile([P, P], U32, align_bytes=64)
-            w_scales = weights.tile([P, P], U8, align_bytes=64)
-            nc.vector.quantize_mx(
-                out=w_codes[:].bitcast(FP8X4), scales=w_scales[:], in_=w_grouped[:]
-            )
-            w_codes_all.append(w_codes)
-            w_scales_all.append(w_scales)
+                nc.tensor.transpose(halves[:, u, :], words[:, u, :], identity[:])
+            return halves
 
-        m_codes_all = []
-        m_scales_all = []
-        for g in range(GROUPS):
+        def turn_q():
+            q_turned = turn(q_rows)
+            q_cols = consts.tile([P, ROWS, PACK], BF16)
+            nc.vector.tensor_copy(
+                out=q_cols[:].rearrange("p r j -> p (r j)").bitcast(F32).rearrange(
+                    "p (r u) -> p r u", u=HALVES
+                ),
+                in_=q_turned[:, :, 0:ROWS].rearrange("p u r -> p r u"),
+            )
+            return q_cols
+
+        def multiply_q(q_cols, g):
             b = g * GROUP // INSTANCES
             shape = [P, GROUP, PIXELS, PACK]
             m_grouped = columns.tile(shape, BF16, align_bytes=64)
@@ -106,6 +96,9 @@ def tile_rpn_modulator_pb_s_kernel(tc, q, feats, po_w, po_b, out):
                 in1=q_cols[:, g * GROUP : (g + 1) * GROUP, :].unsqueeze(2).to_broadcast(shape),
                 op=mybir.AluOpType.mult,
             )
+            return m_grouped
+
+        def quantise_columns(m_grouped):
             m_codes = columns.tile([P, GROUP_COLS], U32, align_bytes=64)
             m_scales = columns.tile([P, GROUP_COLS], U8, align_bytes=64)
             nc.vector.quantize_mx(
@@ -113,25 +106,44 @@ def tile_rpn_modulator_pb_s_kernel(tc, q, feats, po_w, po_b, out):
                 scales=m_scales[:],
                 in_=m_grouped[:].rearrange("p i w j -> p (i w j)"),
             )
-            m_codes_all.append(m_codes)
-            m_scales_all.append(m_scales)
+            return m_codes, m_scales
+
+        def turn_weights(t):
+            w_turned = turn(w_rows_all[t])
+            w_grouped = weights.tile([P, P * PACK], BF16, align_bytes=64)
+            nc.scalar.copy(
+                out=w_grouped[:].bitcast(F32).rearrange("p (m u) -> p m u", u=HALVES),
+                in_=w_turned[:].rearrange("p u m -> p m u"),
+            )
+            return w_grouped
+
+        def quantise_weights(w_grouped):
+            w_codes = weights.tile([P, P], U32, align_bytes=64)
+            w_scales = weights.tile([P, P], U8, align_bytes=64)
+            nc.vector.quantize_mx(
+                out=w_codes[:].bitcast(FP8X4), scales=w_scales[:], in_=w_grouped[:]
+            )
+            return w_codes, w_scales
 
         out_view = out.rearrange("b i (m t) y x -> m (b i) (t y x)", t=O_TILES)
-        for g in range(GROUPS):
+
+        def finish_group(g, w_operands, m_operand):
+            m_codes, m_scales = m_operand
             result = columns.tile([P, GROUP, O_TILES, PIXELS], F32)
             for t in range(O_TILES):
+                w_codes, w_scales = w_operands[t]
                 acc = sums.tile([P, GROUP_COLS], F32)
                 nc.tensor.matmul_mx(
                     out=acc[:],
-                    lhsT=w_codes_all[t][:].bitcast(FP8X4),
-                    lhsT_scale=w_scales_all[t][:],
-                    rhs=m_codes_all[g][:].bitcast(FP8X4),
-                    rhs_scale=m_scales_all[g][:],
+                    lhsT=w_codes[:].bitcast(FP8X4),
+                    lhsT_scale=w_scales[:],
+                    rhs=m_codes[:].bitcast(FP8X4),
+                    rhs_scale=m_scales[:],
                     start=True,
                     stop=True,
                 )
                 acc_view = acc[:].rearrange("m (i w) -> m i w", w=PIXELS)
-                if t % 2 == 0:
+                if t < O_TILES - 1:
                     nc.scalar.activation(
                         out=result[:, :, t, :],
                         in_=acc_view,
@@ -147,3 +159,11 @@ def tile_rpn_modulator_pb_s_kernel(tc, q, feats, po_w, po_b, out):
                 out=out_view[:, g * GROUP : (g + 1) * GROUP, :],
                 in_=result[:].rearrange("m i t w -> m i (t w)"),
             )
+
+        q_cols = turn_q()
+        m_operands = [quantise_columns(multiply_q(q_cols, 0))]
+        w_operands = [quantise_weights(turn_weights(t)) for t in range(O_TILES)]
+        for g in range(GROUPS):
+            if g + 1 < GROUPS:
+                m_operands.append(quantise_columns(multiply_q(q_cols, g + 1)))
+            finish_group(g, w_operands, m_operands[g])

@@ -161,9 +161,14 @@ def tile_rpn_modulator_pb_s_kernel(tc, q, feats, po_w, po_b, out):
             )
 
         q_cols = turn_q()
-        m_operands = [quantise_columns(multiply_q(q_cols, 0))]
-        w_operands = [quantise_weights(turn_weights(t)) for t in range(O_TILES)]
+        w_grouped_all = [turn_weights(t) for t in range(O_TILES)]
+        m_grouped = multiply_q(q_cols, 0)
+        w_operands = [quantise_weights(w_grouped_all[0])]
+        m_operand = quantise_columns(m_grouped)
+        w_operands.extend(quantise_weights(w_grouped_all[t]) for t in range(1, O_TILES))
         for g in range(GROUPS):
             if g + 1 < GROUPS:
-                m_operands.append(quantise_columns(multiply_q(q_cols, g + 1)))
-            finish_group(g, w_operands, m_operands[g])
+                m_grouped = multiply_q(q_cols, g + 1)
+            finish_group(g, w_operands, m_operand)
+            if g + 1 < GROUPS:
+                m_operand = quantise_columns(m_grouped)

@@ -22,6 +22,7 @@ O_TILES = CHANNELS // P
 GROUP = 4
 GROUPS = ROWS // GROUP
 GROUP_COLS = GROUP * PIXELS
+SHARED_FROM = 2
 
 FLOPS = 2 * ROWS * PIXELS * CHANNELS * CHANNELS
 
@@ -39,27 +40,26 @@ def tile_rpn_modulator_pb_s_kernel(tc, q, feats, po_w, po_b, out):
         identity = consts.tile([P, P], F32)
         make_identity(nc, identity[:])
 
+        q_rows = consts.tile([P, CHANNELS], BF16)
+        for k in range(2):
+            nc.sync.dma_start(
+                out=q_rows[k * ROWS : (k + 1) * ROWS, :], in_=q.rearrange("b i c -> (b i) c")
+            )
+        nc.vector.memset(q_rows[2 * ROWS : 4 * ROWS, :], 0.0)
+        nc.vector.memset(q_rows[4 * ROWS : P, :], 0.0)
+        feats_rows = consts.tile([P, IMAGES, PACK * PIXELS], BF16)
+        nc.sync.dma_start(
+            out=feats_rows[:].rearrange("p b (u r) -> p (b u) r", u=HALVES),
+            in_=feats.rearrange("b (u p e) y x -> p (b u) (e y x)", u=HALVES, e=2),
+        )
         w_view = po_w.rearrange("(m t) c -> m t c", t=O_TILES)
         w_rows_all = []
         for t in range(O_TILES):
             w_rows = weights.tile([P, CHANNELS], BF16)
             nc.sync.dma_start(out=w_rows[:], in_=w_view[:, t, :])
             w_rows_all.append(w_rows)
-
-        q_rows = consts.tile([P, CHANNELS], BF16)
-        for k in range(2):
-            nc.scalar.dma_start(
-                out=q_rows[k * ROWS : (k + 1) * ROWS, :], in_=q.rearrange("b i c -> (b i) c")
-            )
-        nc.vector.memset(q_rows[2 * ROWS : 4 * ROWS, :], 0.0)
-        nc.vector.memset(q_rows[4 * ROWS : P, :], 0.0)
-        feats_rows = consts.tile([P, IMAGES, PACK * PIXELS], BF16)
-        nc.scalar.dma_start(
-            out=feats_rows[:].rearrange("p b (u r) -> p (b u) r", u=HALVES),
-            in_=feats.rearrange("b (u p e) y x -> p (b u) (e y x)", u=HALVES, e=2),
-        )
         bias_bf16 = consts.tile([P, O_TILES], BF16)
-        nc.scalar.dma_start(out=bias_bf16[:], in_=po_b.rearrange("(m t) -> m t", t=O_TILES))
+        nc.sync.dma_start(out=bias_bf16[:], in_=po_b.rearrange("(m t) -> m t", t=O_TILES))
         bias = consts.tile([P, O_TILES], F32)
         nc.gpsimd.tensor_copy(out=bias[:], in_=bias_bf16[:])
 
@@ -143,7 +143,7 @@ def tile_rpn_modulator_pb_s_kernel(tc, q, feats, po_w, po_b, out):
                     stop=True,
                 )
                 acc_view = acc[:].rearrange("m (i w) -> m i w", w=PIXELS)
-                if t < O_TILES - 1:
+                if g < SHARED_FROM or t % 2 == 0:
                     nc.scalar.activation(
                         out=result[:, :, t, :],
                         in_=acc_view,
@@ -164,11 +164,9 @@ def tile_rpn_modulator_pb_s_kernel(tc, q, feats, po_w, po_b, out):
         w_grouped_all = [turn_weights(t) for t in range(O_TILES)]
         m_grouped = multiply_q(q_cols, 0)
         w_operands = [quantise_weights(w_grouped_all[0])]
-        m_operand = quantise_columns(m_grouped)
+        m_operands = [quantise_columns(m_grouped)]
         w_operands.extend(quantise_weights(w_grouped_all[t]) for t in range(1, O_TILES))
+        for g in range(1, GROUPS):
+            m_operands.append(quantise_columns(multiply_q(q_cols, g)))
         for g in range(GROUPS):
-            if g + 1 < GROUPS:
-                m_grouped = multiply_q(q_cols, g + 1)
-            finish_group(g, w_operands, m_operand)
-            if g + 1 < GROUPS:
-                m_operand = quantise_columns(m_grouped)
+            finish_group(g, w_operands, m_operands[g])

from contextlib import ExitStack

import concourse.mybir as mybir
from concourse.masks import make_identity

F32 = mybir.dt.float32
BF16 = mybir.dt.bfloat16
U32 = mybir.dt.uint32
U8 = mybir.dt.uint8
FP8X4 = mybir.dt.float8_e4m3fn_x4

P = 128
PACK = 4
HALVES = 2

IMAGES = 2
INSTANCES = 8
CHANNELS = 512
PIXELS = 64
ROWS = IMAGES * INSTANCES
O_TILES = CHANNELS // P
GROUP = 4
GROUPS = ROWS // GROUP
GROUP_COLS = GROUP * PIXELS
SHARED_FROM = 2

FLOPS = 2 * ROWS * PIXELS * CHANNELS * CHANNELS


def tile_rpn_modulator_pb_s_kernel(tc, q, feats, po_w, po_b, out):
    nc = tc.nc
    with ExitStack() as ctx:
        consts = ctx.enter_context(tc.tile_pool(name="consts", bufs=1))
        weights = ctx.enter_context(tc.tile_pool(name="weights", bufs=O_TILES))
        columns = ctx.enter_context(tc.tile_pool(name="columns", bufs=GROUPS))
        turned = ctx.enter_context(tc.psum_pool(name="turned", bufs=4))
        sums = ctx.enter_context(tc.psum_pool(name="sums", bufs=4))
        ctx.enter_context(tc.manual_schedule())

        identity = consts.tile([P, P], F32)
        make_identity(nc, identity[:])

        q_rows = consts.tile([P, CHANNELS], BF16)
        for k in range(2):
            nc.sync.dma_start(
                out=q_rows[k * ROWS : (k + 1) * ROWS, :], in_=q.rearrange("b i c -> (b i) c")
            )
        nc.vector.memset(q_rows[2 * ROWS : 4 * ROWS, :], 0.0)
        nc.vector.memset(q_rows[4 * ROWS : P, :], 0.0)
        feats_rows = consts.tile([P, IMAGES, PACK * PIXELS], BF16)
        nc.sync.dma_start(
            out=feats_rows[:].rearrange("p b (u r) -> p (b u) r", u=HALVES),
            in_=feats.rearrange("b (u p e) y x -> p (b u) (e y x)", u=HALVES, e=2),
        )
        w_view = po_w.rearrange("(m t) c -> m t c", t=O_TILES)
        w_rows_all = []
        for t in range(O_TILES):
            w_rows = weights.tile([P, CHANNELS], BF16)
            nc.sync.dma_start(out=w_rows[:], in_=w_view[:, t, :])
            w_rows_all.append(w_rows)
        bias_bf16 = consts.tile([P, O_TILES], BF16)
        nc.sync.dma_start(out=bias_bf16[:], in_=po_b.rearrange("(m t) -> m t", t=O_TILES))
        bias = consts.tile([P, O_TILES], F32)
        nc.gpsimd.tensor_copy(out=bias[:], in_=bias_bf16[:])

        feats_grouped = consts.tile([P, IMAGES, PIXELS, PACK], BF16)
        nc.vector.tensor_copy(
            out=feats_grouped[:], in_=feats_rows[:].rearrange("p b (j w) -> p b w j", j=PACK)
        )

        def turn(rows):
            words = rows[:].bitcast(F32).rearrange("r (u p) -> r u p", u=HALVES)
            halves = turned.tile([P, HALVES, P], F32)
            for u in range(HALVES):
                nc.tensor.transpose(halves[:, u, :], words[:, u, :], identity[:])
            return halves

        def turn_q():
            q_turned = turn(q_rows)
            q_cols = consts.tile([P, ROWS, PACK], BF16)
            nc.vector.tensor_copy(
                out=q_cols[:].rearrange("p r j -> p (r j)").bitcast(F32).rearrange(
                    "p (r u) -> p r u", u=HALVES
                ),
                in_=q_turned[:, :, 0:ROWS].rearrange("p u r -> p r u"),
            )
            return q_cols

        def multiply_q(q_cols, g):
            b = g * GROUP // INSTANCES
            shape = [P, GROUP, PIXELS, PACK]
            m_grouped = columns.tile(shape, BF16, align_bytes=64)
            nc.vector.tensor_tensor(
                out=m_grouped[:],
                in0=feats_grouped[:, b].unsqueeze(1).to_broadcast(shape),
                in1=q_cols[:, g * GROUP : (g + 1) * GROUP, :].unsqueeze(2).to_broadcast(shape),
                op=mybir.AluOpType.mult,
            )
            return m_grouped

        def quantise_columns(m_grouped):
            m_codes = columns.tile([P, GROUP_COLS], U32, align_bytes=64)
            m_scales = columns.tile([P, GROUP_COLS], U8, align_bytes=64)
            nc.vector.quantize_mx(
                out=m_codes[:].bitcast(FP8X4),
                scales=m_scales[:],
                in_=m_grouped[:].rearrange("p i w j -> p (i w j)"),
            )
            return m_codes, m_scales

        def turn_weights(t):
            w_turned = turn(w_rows_all[t])
            w_grouped = weights.tile([P, P * PACK], BF16, align_bytes=64)
            nc.scalar.copy(
                out=w_grouped[:].bitcast(F32).rearrange("p (m u) -> p m u", u=HALVES),
                in_=w_turned[:].rearrange("p u m -> p m u"),
            )
            return w_grouped

        def quantise_weights(w_grouped):
            w_codes = weights.tile([P, P], U32, align_bytes=64)
            w_scales = weights.tile([P, P], U8, align_bytes=64)
            nc.vector.quantize_mx(
                out=w_codes[:].bitcast(FP8X4), scales=w_scales[:], in_=w_grouped[:]
            )
            return w_codes, w_scales

        out_view = out.rearrange("b i (m t) y x -> m (b i) (t y x)", t=O_TILES)

        def finish_group(g, w_operands, m_operand):
            m_codes, m_scales = m_operand
            result = columns.tile([P, GROUP, O_TILES, PIXELS], F32)
            for t in range(O_TILES):
                w_codes, w_scales = w_operands[t]
                acc = sums.tile([P, GROUP_COLS], F32)
                nc.tensor.matmul_mx(
                    out=acc[:],
                    lhsT=w_codes[:].bitcast(FP8X4),
                    lhsT_scale=w_scales[:],
                    rhs=m_codes[:].bitcast(FP8X4),
                    rhs_scale=m_scales[:],
                    start=True,
                    stop=True,
                )
                acc_view = acc[:].rearrange("m (i w) -> m i w", w=PIXELS)
                if g < SHARED_FROM or t % 2 == 0:
                    nc.scalar.activation(
                        out=result[:, :, t, :],
                        in_=acc_view,
                        func=mybir.ActivationFunctionType.Identity,
                        bias=bias[:, t : t + 1],
                        scale=1.0,
                    )
                else:
                    nc.vector.tensor_scalar_add(
                        out=result[:, :, t, :], in0=acc_view, scalar1=bias[:, t : t + 1]
                    )
            nc.sync.dma_start(
                out=out_view[:, g * GROUP : (g + 1) * GROUP, :],
                in_=result[:].rearrange("m i t w -> m i (t w)"),
            )

        q_cols = turn_q()
        w_grouped_all = [turn_weights(t) for t in range(O_TILES)]
        m_grouped = multiply_q(q_cols, 0)
        w_operands = [quantise_weights(w_grouped_all[0])]
        m_operands = [quantise_columns(m_grouped)]
        w_operands.extend(quantise_weights(w_grouped_all[t]) for t in range(1, O_TILES))
        for g in range(1, GROUPS):
            m_operands.append(quantise_columns(multiply_q(q_cols, g)))
        for g in range(GROUPS):
            finish_group(g, w_operands, m_operands[g])
